import numpy as np
import ml_dtypes


def mxq(x, axis, fmt="e4m3"):
    dtype, down = {"e4m3": (ml_dtypes.float8_e4m3fn, 7), "e5m2": (ml_dtypes.float8_e5m2, 14)}[fmt]
    v = np.moveaxis(np.asarray(x, np.float32).astype(ml_dtypes.bfloat16).astype(np.float64), axis, -1)
    blocks = v.reshape(v.shape[:-1] + (-1, 32))
    amax = np.abs(blocks).max(-1, keepdims=True)
    byte = np.maximum(np.where(amax > 0, np.frexp(amax)[1] - 1 + 127, 0) - down, 1)
    scale = np.exp2(byte - 127.0)
    codes = (blocks / scale).astype(np.float32).astype(dtype).astype(np.float64)
    return np.moveaxis((codes * scale).reshape(v.shape), -1, axis)


WIDE = False


def mx_kscale(k):
    if not WIDE:
        return np.ones(k)
    levels = np.array([10, -10, 5, -5, 0])
    a = np.random.permutation(np.resize(levels, k // 512 * 4)).reshape(k // 512, 4)
    idx = np.arange(k)
    return np.exp2(a[idx // 512, idx % 128 // 32])


BF16 = ml_dtypes.bfloat16


def bf(x):
    return np.asarray(x, np.float32).astype(BF16)


def f64(x):
    return np.asarray(x).astype(np.float64)


E2M1 = np.array([0.0, 0.5, 1.0, 1.5, 2.0, 3.0, 4.0, 6.0, -0.0, -0.5, -1.0, -1.5, -2.0, -3.0, -4.0, -6.0])


def pack_weight(w, fmt):
    k, n = w.shape
    w = f64(bf(w)).reshape(k // 32, 32, n)
    amax = np.abs(w).max(1)
    if fmt == "e4m3":
        byte = np.frexp(amax)[1] - 1 + 127 - 7
    else:
        mant, ex = np.frexp(amax / 6.0)
        byte = np.where(mant > 0.5, ex, ex - 1) + 127
    byte = np.clip(np.where(amax > 0, byte, 1), 1, 254)
    scaled = (w * np.exp2(127.0 - byte)[:, None, :]).reshape(k, n).astype(np.float32)
    by_word = np.ascontiguousarray(scaled.reshape(k // 512, 128, 4, n).transpose(0, 1, 3, 2))
    if fmt == "e4m3":
        words = by_word.astype(ml_dtypes.float8_e4m3fn).view(np.uint8)
    else:
        c = by_word.astype(ml_dtypes.float4_e2m1fn).view(np.uint8) & 0xF
        words = c[..., 0::2] | (c[..., 1::2] << 4)
    return np.ascontiguousarray(words), np.ascontiguousarray(byte.astype(np.uint8).reshape(k // 512, 16, n))


def unpack_weight(words, scales, fmt):
    g, p, n, _ = words.shape
    if fmt == "e4m3":
        vals = np.ascontiguousarray(words).view(ml_dtypes.float8_e4m3fn).astype(np.float64)
    else:
        nib = np.empty((g, p, n, 4), np.uint8)
        nib[..., 0::2] = words & 0xF
        nib[..., 1::2] = words >> 4
        vals = E2M1[nib]
    vals = vals * np.repeat(np.exp2(scales.astype(np.float64) - 127.0), 8, axis=1)[..., None]
    return vals.transpose(0, 1, 3, 2).reshape(g * 512, n)

def pack4(w):
    words, scales = pack_weight(w, "e2m1")
    return words.reshape(words.shape[0], 128, -1), scales


def unpack4(words, scales):
    return unpack_weight(words.reshape(words.shape[0], 128, -1, 2), scales, "e2m1")


B, N, NODE_IN, EDGE_IN, EDGE_OUT = 2, 16, 192, 128, 512
D_IN = 2 * NODE_IN + EDGE_IN
HID = 2 * EDGE_OUT
NEG_SLOPE = 0.1


def leaky_relu(v):
    return np.where(v >= 0.0, v, NEG_SLOPE * v)


def setup_inputs():
    s = mx_kscale(D_IN)
    sn, se = s[:NODE_IN], s[2 * NODE_IN:]
    st = np.concatenate([sn, sn, se])
    node_fts = bf(np.random.standard_normal((B, N, NODE_IN)) * sn)
    edge_fts = bf(np.random.standard_normal((B, N * N, EDGE_IN)) * se)
    wt = np.random.standard_normal((HID, D_IN)) / np.sqrt(D_IN) / st
    words, scales = pack4(np.ascontiguousarray(wt.T))
    return {"node_fts": node_fts,
            "edge_fts": edge_fts,
            "Wt_words": words,
            "Wt_scales": scales}


def reference(node_fts, edge_fts, Wt_words, Wt_scales):
    node = f64(node_fts)
    src = np.repeat(node, N, axis=1)
    dst = np.tile(node, (1, N, 1))
    triplet = np.concatenate([src, dst, f64(edge_fts)], axis=-1)
    return leaky_relu(mxq(triplet, 2, "e4m3") @ unpack4(Wt_words, Wt_scales))

@@ -1,0 +1,153 @@
+import concourse.mybir as mybir
+from concourse.masks import make_identity
+
+F32 = mybir.dt.float32
+BF16 = mybir.dt.bfloat16
+I32 = mybir.dt.int32
+U32 = mybir.dt.uint32
+U8 = mybir.dt.uint8
+FP8X4 = mybir.dt.float8_e4m3fn_x4
+FP4X4 = mybir.dt.float4_e2m1fn_x4
+
+P = 128
+GRAPHS = 2
+NODES = 16
+NODE_IN = 192
+EDGE_IN = 128
+D_IN = 2 * NODE_IN + EDGE_IN
+HID = 1024
+NEG_SLOPE = 0.1
+
+ROWS = GRAPHS * NODES * NODES
+TILES = ROWS // P
+HALF_P = P // GRAPHS
+BANK = 512
+FIRST_TILE = (128, 128, 256, BANK)
+MIDDLE_TILE = (BANK, BANK)
+LAST_TILE = (BANK, BANK)
+WORDS = D_IN // 2
+WARM_UP_PASSES = 5
+LIVE_ROWS = 4
+SRC = slice(0, NODE_IN)
+DST = slice(NODE_IN, 2 * NODE_IN)
+EDGE = slice(2 * NODE_IN, D_IN)
+
+FLOPS = 2 * ROWS * D_IN * HID
+
+
+def tile_edge_update_only_pa_s_kernel(tc, node_fts, edge_fts, Wt_words, Wt_scales, out):
+    nc = tc.nc
+    nodes = node_fts.flatten_outer_dims()
+    edge_rows = edge_fts.flatten_outer_dims().rearrange("(p t) f -> p (t f)", t=TILES)
+    out_rows = out.flatten_outer_dims().rearrange("(p t) n -> p t n", t=TILES)
+
+    with tc.tile_pool(name="keep", bufs=1) as keep, tc.tile_pool(
+        name="stage", bufs=TILES
+    ) as stage, tc.tile_pool(name="results", bufs=len(FIRST_TILE) + len(LAST_TILE) + (TILES - 2) * len(MIDDLE_TILE)) as results, tc.psum_pool(
+        name="psum", bufs=8
+    ) as psum:
+        first = keep.tile([P, D_IN + (TILES - 1) * EDGE_IN], BF16)
+        later = keep.tile([P, TILES - 1, D_IN], BF16)
+        dst_nodes = keep.tile([P, TILES, NODE_IN], BF16)
+        w_words = keep.tile([P, 2 * HID], U8, align_bytes=64)
+        w_scales = keep.tile([P, HID], U8, align_bytes=64)
+        t_codes = keep.tile([P, TILES, P], U32, align_bytes=64)
+        t_scales = keep.tile([P, TILES, P], U8, align_bytes=64)
+        identity = keep.tile([P, P], F32)
+        idle_work = keep.tile([P, P], F32)
+
+        def load_triplets():
+            nc.sync.dma_start(
+                out=first[:, SRC],
+                in_=nodes.unsqueeze(1).to_broadcast([GRAPHS * NODES, NODES // TILES, NODE_IN]),
+            )
+            for b in range(GRAPHS):
+                nc.sync.dma_start(
+                    out=dst_nodes[HALF_P * b : HALF_P * (b + 1), :, :].rearrange("p t f -> p (t f)"),
+                    in_=node_fts[b]
+                    .rearrange("(q t) f -> q (t f)", t=TILES)
+                    .unsqueeze(0)
+                    .to_broadcast([NODES, NODES // TILES, TILES * NODE_IN]),
+                )
+            nc.sync.dma_start(out=first[:, 2 * NODE_IN :], in_=edge_rows)
+
+        def load_weight():
+            nc.sync.dma_start(out=w_words[:].bitcast(I32), in_=Wt_words[0].bitcast(I32))
+            for q in range(P // 32):
+                nc.sync.dma_start(
+                    out=w_scales[32 * q : 32 * q + LIVE_ROWS, :].bitcast(I32),
+                    in_=Wt_scales[0, LIVE_ROWS * q : LIVE_ROWS * (q + 1), :].bitcast(I32),
+                )
+
+        def assemble_triplets():
+            nc.vector.tensor_copy(out=first[:, DST], in_=dst_nodes[:, 0, :])
+            nc.scalar.copy(out=later[:, :, EDGE], in_=first[:, D_IN:].rearrange("p (t f) -> p t f", f=EDGE_IN))
+            nc.vector.tensor_copy(out=later[:, :, DST], in_=dst_nodes[:, 1:TILES, :])
+            nc.vector.tensor_copy(
+                out=later[:, :, SRC],
+                in_=first[:, SRC].unsqueeze(1).to_broadcast([P, TILES - 1, NODE_IN]),
+            )
+
+        def quantise_tile(t):
+            words = (first[:, 0:D_IN] if t == 0 else later[:, t - 1, :]).bitcast(F32)
+            flipped = psum.tile([P, BANK], F32, tag="bank")
+            planes = flipped[:, 0:WORDS].rearrange("p (u m) -> p u m", u=2)
+            for u in range(2):
+                nc.tensor.transpose(planes[:, u, :], words[:, u:WORDS:2], identity[:])
+            grouped = stage.tile([P, 4 * P], BF16, align_bytes=64)
+            nc.scalar.copy(
+                out=grouped[:].bitcast(F32).rearrange("p (m u) -> p m u", u=2),
+                in_=planes.rearrange("p u m -> p m u"),
+            )
+            nc.vector.quantize_mx(
+                out=t_codes[:, t, :].bitcast(FP8X4), scales=t_scales[:, t, :], in_=grouped[:]
+            )
+
+        def multiply_tile(t, widths):
+            first = 0
+            for width in widths:
+                last = first + width
+                acc = psum.tile([P, BANK], F32, tag="bank")
+                nc.tensor.matmul_mx(
+                    out=acc[:, 0:width],
+                    lhsT=t_codes[:, t, :].bitcast(FP8X4),
+                    lhsT_scale=t_scales[:, t, :],
+                    rhs=w_words[:, 2 * first : 2 * last].bitcast(FP4X4),
+                    rhs_scale=w_scales[:, first:last],
+                    start=True,
+                    stop=True,
+                )
+                tenth = stage.tile([P, BANK], F32)
+                nc.scalar.mul(out=tenth[:, 0:width], in_=acc[:, 0:width], mul=NEG_SLOPE)
+                result = results.tile([P, BANK], F32)
+                nc.vector.tensor_max(result[:, 0:width], acc[:, 0:width], tenth[:, 0:width])
+                nc.sync.dma_start(out=out_rows[:, t, first:last], in_=result[:, 0:width])
+                first = last
+
+        def keep_warm():
+            unused = psum.tile([P, BANK], F32, tag="bank")
+            nc.tensor.matmul(out=unused[:, 0:P], lhsT=idle_work[:], rhs=idle_work[:], start=True, stop=True)
+
+        def warm_up():
+            nc.gpsimd.memset(idle_work[:], 0.0)
+            unused = psum.tile([P, BANK], F32, tag="bank")
+            for _ in range(WARM_UP_PASSES):
+                nc.tensor.matmul(out=unused[:, 0:P], lhsT=idle_work[:], rhs=idle_work[:], start=True, stop=True)
+
+        def run():
+            nc.vector.memset(w_scales[:].bitcast(I32), 0)
+            warm_up()
+            make_identity(nc, identity[:])
+            load_triplets()
+            load_weight()
+            assemble_triplets()
+            for t in range(TILES):
+                quantise_tile(t)
+            keep_warm()
+            multiply_tile(0, FIRST_TILE)
+            for t in range(1, TILES - 1):
+                multiply_tile(t, MIDDLE_TILE)
+            multiply_tile(TILES - 1, LAST_TILE)
+
+        with tc.manual_schedule(engines={mybir.EngineType.PE}):
+            run()

@@ -26,7 +26,7 @@ FIRST_TILE = (128, 128, 256, BANK)
 MIDDLE_TILE = (BANK, BANK)
 LAST_TILE = (BANK, BANK)
 WORDS = D_IN // 2
-WARM_UP_PASSES = 5
+WARM_UP_PASSES = 4
 LIVE_ROWS = 4
 SRC = slice(0, NODE_IN)
 DST = slice(NODE_IN, 2 * NODE_IN)
@@ -48,7 +48,7 @@ def tile_edge_update_only_pa_s_kernel(tc, node_fts, edge_fts, Wt_words, Wt_scale
     ) as psum:
         first = keep.tile([P, D_IN + (TILES - 1) * EDGE_IN], BF16)
         later = keep.tile([P, TILES - 1, D_IN], BF16)
-        dst_nodes = keep.tile([P, TILES, NODE_IN], BF16)
+        dst_nodes = keep.tile([P, TILES - 1, NODE_IN], BF16)
         w_words = keep.tile([P, 2 * HID], U8, align_bytes=64)
         w_scales = keep.tile([P, HID], U8, align_bytes=64)
         t_codes = keep.tile([P, TILES, P], U32, align_bytes=64)
@@ -61,15 +61,20 @@ def tile_edge_update_only_pa_s_kernel(tc, node_fts, edge_fts, Wt_words, Wt_scale
                 out=first[:, SRC],
                 in_=nodes.unsqueeze(1).to_broadcast([GRAPHS * NODES, NODES // TILES, NODE_IN]),
             )
+            def destinations(b, columns):
+                rows = node_fts[b].rearrange("(q t) f -> q (t f)", t=TILES)[:, columns]
+                return rows.unsqueeze(0).to_broadcast([NODES, NODES // TILES, columns.stop - columns.start])
+
+            for b in range(GRAPHS):
+                nc.sync.dma_start(
+                    out=first[HALF_P * b : HALF_P * (b + 1), DST], in_=destinations(b, slice(0, NODE_IN))
+                )
+            nc.sync.dma_start(out=first[:, 2 * NODE_IN :], in_=edge_rows)
             for b in range(GRAPHS):
                 nc.sync.dma_start(
                     out=dst_nodes[HALF_P * b : HALF_P * (b + 1), :, :].rearrange("p t f -> p (t f)"),
-                    in_=node_fts[b]
-                    .rearrange("(q t) f -> q (t f)", t=TILES)
-                    .unsqueeze(0)
-                    .to_broadcast([NODES, NODES // TILES, TILES * NODE_IN]),
+                    in_=destinations(b, slice(NODE_IN, TILES * NODE_IN)),
                 )
-            nc.sync.dma_start(out=first[:, 2 * NODE_IN :], in_=edge_rows)
 
         def load_weight():
             nc.sync.dma_start(out=w_words[:].bitcast(I32), in_=Wt_words[0].bitcast(I32))
@@ -80,30 +85,35 @@ def tile_edge_update_only_pa_s_kernel(tc, node_fts, edge_fts, Wt_words, Wt_scale
                 )
 
         def assemble_triplets():
-            nc.vector.tensor_copy(out=first[:, DST], in_=dst_nodes[:, 0, :])
-            nc.scalar.copy(out=later[:, :, EDGE], in_=first[:, D_IN:].rearrange("p (t f) -> p t f", f=EDGE_IN))
-            nc.vector.tensor_copy(out=later[:, :, DST], in_=dst_nodes[:, 1:TILES, :])
             nc.vector.tensor_copy(
                 out=later[:, :, SRC],
                 in_=first[:, SRC].unsqueeze(1).to_broadcast([P, TILES - 1, NODE_IN]),
             )
+            nc.vector.tensor_copy(out=later[:, :, EDGE], in_=first[:, D_IN:].rearrange("p (t f) -> p t f", f=EDGE_IN))
+            nc.vector.tensor_copy(out=later[:, :, DST], in_=dst_nodes[:])
 
-        def quantise_tile(t):
+        def transpose_tile(t):
             words = (first[:, 0:D_IN] if t == 0 else later[:, t - 1, :]).bitcast(F32)
             flipped = psum.tile([P, BANK], F32, tag="bank")
             planes = flipped[:, 0:WORDS].rearrange("p (u m) -> p u m", u=2)
             for u in range(2):
                 nc.tensor.transpose(planes[:, u, :], words[:, u:WORDS:2], identity[:])
+            return planes
+
+        def group_words(copy, planes):
             grouped = stage.tile([P, 4 * P], BF16, align_bytes=64)
-            nc.scalar.copy(
+            copy(
                 out=grouped[:].bitcast(F32).rearrange("p (m u) -> p m u", u=2),
                 in_=planes.rearrange("p u m -> p m u"),
             )
+            return grouped
+
+        def quantise_tile(t, grouped):
             nc.vector.quantize_mx(
                 out=t_codes[:, t, :].bitcast(FP8X4), scales=t_scales[:, t, :], in_=grouped[:]
             )
 
-        def multiply_tile(t, widths):
+        def multiply_tile(t, widths, after_second=None):
             first = 0
             for width in widths:
                 last = first + width
@@ -123,10 +133,8 @@ def tile_edge_update_only_pa_s_kernel(tc, node_fts, edge_fts, Wt_words, Wt_scale
                 nc.vector.tensor_max(result[:, 0:width], acc[:, 0:width], tenth[:, 0:width])
                 nc.sync.dma_start(out=out_rows[:, t, first:last], in_=result[:, 0:width])
                 first = last
-
-        def keep_warm():
-            unused = psum.tile([P, BANK], F32, tag="bank")
-            nc.tensor.matmul(out=unused[:, 0:P], lhsT=idle_work[:], rhs=idle_work[:], start=True, stop=True)
+                if after_second is not None and last == 2 * P:
+                    after_second()
 
         def warm_up():
             nc.gpsimd.memset(idle_work[:], 0.0)
@@ -141,13 +149,16 @@ def tile_edge_update_only_pa_s_kernel(tc, node_fts, edge_fts, Wt_words, Wt_scale
             load_triplets()
             load_weight()
             assemble_triplets()
-            for t in range(TILES):
-                quantise_tile(t)
-            keep_warm()
-            multiply_tile(0, FIRST_TILE)
+            planes = [transpose_tile(t) for t in range(TILES)]
+            quantise_tile(0, group_words(nc.vector.tensor_copy, planes[0]))
+            quantise_tile(1, group_words(nc.scalar.copy, planes[1]))
+            grouped_2 = group_words(nc.scalar.copy, planes[2])
+            grouped_3 = group_words(nc.vector.tensor_copy, planes[3])
+            quantise_tile(2, grouped_2)
+            multiply_tile(0, FIRST_TILE, after_second=lambda: quantise_tile(3, grouped_3))
             for t in range(1, TILES - 1):
                 multiply_tile(t, MIDDLE_TILE)
             multiply_tile(TILES - 1, LAST_TILE)
 
-        with tc.manual_schedule(engines={mybir.EngineType.PE}):
+        with tc.manual_schedule(engines={mybir.EngineType.PE, mybir.EngineType.DVE}):
             run()

@@ -26,7 +26,7 @@ FIRST_TILE = (128, 128, 256, BANK)
 MIDDLE_TILE = (BANK, BANK)
 LAST_TILE = (BANK, BANK)
 WORDS = D_IN // 2
-WARM_UP_PASSES = 4
+WARM_UP_PASSES = 3
 LIVE_ROWS = 4
 SRC = slice(0, NODE_IN)
 DST = slice(NODE_IN, 2 * NODE_IN)
@@ -48,7 +48,7 @@ def tile_edge_update_only_pa_s_kernel(tc, node_fts, edge_fts, Wt_words, Wt_scale
     ) as psum:
         first = keep.tile([P, D_IN + (TILES - 1) * EDGE_IN], BF16)
         later = keep.tile([P, TILES - 1, D_IN], BF16)
-        dst_nodes = keep.tile([P, TILES - 1, NODE_IN], BF16)
+        pick = keep.tile([P, TILES - 1, P], BF16)
         w_words = keep.tile([P, 2 * HID], U8, align_bytes=64)
         w_scales = keep.tile([P, HID], U8, align_bytes=64)
         t_codes = keep.tile([P, TILES, P], U32, align_bytes=64)
@@ -61,20 +61,37 @@ def tile_edge_update_only_pa_s_kernel(tc, node_fts, edge_fts, Wt_words, Wt_scale
                 out=first[:, SRC],
                 in_=nodes.unsqueeze(1).to_broadcast([GRAPHS * NODES, NODES // TILES, NODE_IN]),
             )
-            def destinations(b, columns):
-                rows = node_fts[b].rearrange("(q t) f -> q (t f)", t=TILES)[:, columns]
-                return rows.unsqueeze(0).to_broadcast([NODES, NODES // TILES, columns.stop - columns.start])
-
             for b in range(GRAPHS):
                 nc.sync.dma_start(
-                    out=first[HALF_P * b : HALF_P * (b + 1), DST], in_=destinations(b, slice(0, NODE_IN))
+                    out=first[HALF_P * b : HALF_P * (b + 1), DST],
+                    in_=node_fts[b]
+                    .rearrange("(q t) f -> q t f", t=TILES)[:, 0, :]
+                    .unsqueeze(0)
+                    .to_broadcast([NODES, NODES // TILES, NODE_IN]),
                 )
             nc.sync.dma_start(out=first[:, 2 * NODE_IN :], in_=edge_rows)
-            for b in range(GRAPHS):
-                nc.sync.dma_start(
-                    out=dst_nodes[HALF_P * b : HALF_P * (b + 1), :, :].rearrange("p t f -> p (t f)"),
-                    in_=destinations(b, slice(NODE_IN, TILES * NODE_IN)),
+
+        def make_picks():
+            for t in range(1, TILES):
+                nc.vector.tensor_copy(
+                    out=pick[:, t - 1, :].rearrange("n (b i q) -> n b i q", b=GRAPHS, q=TILES),
+                    in_=identity[:]
+                    .rearrange("n (b q t c) -> n t c b q", b=GRAPHS, q=TILES, t=TILES)[:, t, 0]
+                    .unsqueeze(2)
+                    .to_broadcast([P, GRAPHS, NODES, TILES]),
                 )
+
+        def pick_destinations(tiles):
+            picked = psum.tile([P, 2 * BANK], BF16, tag="bank")
+            for n, t in enumerate(tiles):
+                nc.tensor.matmul(
+                    out=picked[:, NODE_IN * n : NODE_IN * (n + 1)],
+                    lhsT=pick[:, t - 1, :],
+                    rhs=first[:, SRC],
+                    start=True,
+                    stop=True,
+                )
+            return picked
 
         def load_weight():
             nc.sync.dma_start(out=w_words[:].bitcast(I32), in_=Wt_words[0].bitcast(I32))
@@ -90,7 +107,11 @@ def tile_edge_update_only_pa_s_kernel(tc, node_fts, edge_fts, Wt_words, Wt_scale
                 in_=first[:, SRC].unsqueeze(1).to_broadcast([P, TILES - 1, NODE_IN]),
             )
             nc.vector.tensor_copy(out=later[:, :, EDGE], in_=first[:, D_IN:].rearrange("p (t f) -> p t f", f=EDGE_IN))
-            nc.vector.tensor_copy(out=later[:, :, DST], in_=dst_nodes[:])
+            picked_1, picked_23 = pick_destinations((1,)), pick_destinations((2, 3))
+            nc.scalar.copy(out=later[:, 0, DST], in_=picked_1[:, 0:NODE_IN])
+            nc.scalar.copy(
+                out=later[:, 1:3, DST], in_=picked_23[:, 0 : 2 * NODE_IN].rearrange("p (t f) -> p t f", f=NODE_IN)
+            )
 
         def transpose_tile(t):
             words = (first[:, 0:D_IN] if t == 0 else later[:, t - 1, :]).bitcast(F32)
@@ -146,6 +167,7 @@ def tile_edge_update_only_pa_s_kernel(tc, node_fts, edge_fts, Wt_words, Wt_scale
             nc.vector.memset(w_scales[:].bitcast(I32), 0)
             warm_up()
             make_identity(nc, identity[:])
+            make_picks()
             load_triplets()
             load_weight()
             assemble_triplets()

@@ -106,12 +106,11 @@ def tile_edge_update_only_pa_s_kernel(tc, node_fts, edge_fts, Wt_words, Wt_scale
                 out=later[:, :, SRC],
                 in_=first[:, SRC].unsqueeze(1).to_broadcast([P, TILES - 1, NODE_IN]),
             )
+            for t in range(1, TILES):
+                picked = pick_destinations((t,))
+                copy = nc.vector.tensor_copy if t == 1 else nc.scalar.copy
+                copy(out=later[:, t - 1, DST], in_=picked[:, 0:NODE_IN])
             nc.vector.tensor_copy(out=later[:, :, EDGE], in_=first[:, D_IN:].rearrange("p (t f) -> p t f", f=EDGE_IN))
-            picked_1, picked_23 = pick_destinations((1,)), pick_destinations((2, 3))
-            nc.scalar.copy(out=later[:, 0, DST], in_=picked_1[:, 0:NODE_IN])
-            nc.scalar.copy(
-                out=later[:, 1:3, DST], in_=picked_23[:, 0 : 2 * NODE_IN].rearrange("p (t f) -> p t f", f=NODE_IN)
-            )
 
         def transpose_tile(t):
             words = (first[:, 0:D_IN] if t == 0 else later[:, t - 1, :]).bitcast(F32)
@@ -157,6 +156,10 @@ def tile_edge_update_only_pa_s_kernel(tc, node_fts, edge_fts, Wt_words, Wt_scale
                 if after_second is not None and last == 2 * P:
                     after_second()
 
+        def keep_warm():
+            unused = psum.tile([P, BANK], F32, tag="bank")
+            nc.tensor.matmul(out=unused[:, 0:P], lhsT=idle_work[:], rhs=idle_work[:], start=True, stop=True)
+
         def warm_up():
             nc.gpsimd.memset(idle_work[:], 0.0)
             unused = psum.tile([P, BANK], F32, tag="bank")
@@ -171,7 +174,9 @@ def tile_edge_update_only_pa_s_kernel(tc, node_fts, edge_fts, Wt_words, Wt_scale
             load_triplets()
             load_weight()
             assemble_triplets()
-            planes = [transpose_tile(t) for t in range(TILES)]
+            planes = [transpose_tile(0)]
+            keep_warm()
+            planes += [transpose_tile(t) for t in range(1, TILES)]
             quantise_tile(0, group_words(nc.vector.tensor_copy, planes[0]))
             quantise_tile(1, group_words(nc.scalar.copy, planes[1]))
             grouped_2 = group_words(nc.scalar.copy, planes[2])

import concourse.mybir as mybir
from concourse.masks import make_identity

F32 = mybir.dt.float32
BF16 = mybir.dt.bfloat16
I32 = mybir.dt.int32
U32 = mybir.dt.uint32
U8 = mybir.dt.uint8
FP8X4 = mybir.dt.float8_e4m3fn_x4
FP4X4 = mybir.dt.float4_e2m1fn_x4

P = 128
GRAPHS = 2
NODES = 16
NODE_IN = 192
EDGE_IN = 128
D_IN = 2 * NODE_IN + EDGE_IN
HID = 1024
NEG_SLOPE = 0.1

ROWS = GRAPHS * NODES * NODES
TILES = ROWS // P
HALF_P = P // GRAPHS
BANK = 512
FIRST_TILE = (128, 128, 256, BANK)
MIDDLE_TILE = (BANK, BANK)
LAST_TILE = (BANK, BANK)
WORDS = D_IN // 2
WARM_UP_PASSES = 3
LIVE_ROWS = 4
SRC = slice(0, NODE_IN)
DST = slice(NODE_IN, 2 * NODE_IN)
EDGE = slice(2 * NODE_IN, D_IN)

FLOPS = 2 * ROWS * D_IN * HID


def tile_edge_update_only_pa_s_kernel(tc, node_fts, edge_fts, Wt_words, Wt_scales, out):
    nc = tc.nc
    nodes = node_fts.flatten_outer_dims()
    edge_rows = edge_fts.flatten_outer_dims().rearrange("(p t) f -> p (t f)", t=TILES)
    out_rows = out.flatten_outer_dims().rearrange("(p t) n -> p t n", t=TILES)

    with tc.tile_pool(name="keep", bufs=1) as keep, tc.tile_pool(
        name="stage", bufs=TILES
    ) as stage, tc.tile_pool(name="results", bufs=len(FIRST_TILE) + len(LAST_TILE) + (TILES - 2) * len(MIDDLE_TILE)) as results, tc.psum_pool(
        name="psum", bufs=8
    ) as psum:
        first = keep.tile([P, D_IN + (TILES - 1) * EDGE_IN], BF16)
        later = keep.tile([P, TILES - 1, D_IN], BF16)
        pick = keep.tile([P, TILES - 1, P], BF16)
        w_words = keep.tile([P, 2 * HID], U8, align_bytes=64)
        w_scales = keep.tile([P, HID], U8, align_bytes=64)
        t_codes = keep.tile([P, TILES, P], U32, align_bytes=64)
        t_scales = keep.tile([P, TILES, P], U8, align_bytes=64)
        identity = keep.tile([P, P], F32)
        idle_work = keep.tile([P, P], F32)

        def load_triplets():
            nc.sync.dma_start(
                out=first[:, SRC],
                in_=nodes.unsqueeze(1).to_broadcast([GRAPHS * NODES, NODES // TILES, NODE_IN]),
            )
            for b in range(GRAPHS):
                nc.sync.dma_start(
                    out=first[HALF_P * b : HALF_P * (b + 1), DST],
                    in_=node_fts[b]
                    .rearrange("(q t) f -> q t f", t=TILES)[:, 0, :]
                    .unsqueeze(0)
                    .to_broadcast([NODES, NODES // TILES, NODE_IN]),
                )
            nc.sync.dma_start(out=first[:, 2 * NODE_IN :], in_=edge_rows)

        def make_picks():
            for t in range(1, TILES):
                nc.vector.tensor_copy(
                    out=pick[:, t - 1, :].rearrange("n (b i q) -> n b i q", b=GRAPHS, q=TILES),
                    in_=identity[:]
                    .rearrange("n (b q t c) -> n t c b q", b=GRAPHS, q=TILES, t=TILES)[:, t, 0]
                    .unsqueeze(2)
                    .to_broadcast([P, GRAPHS, NODES, TILES]),
                )

        def pick_destinations(tiles):
            picked = psum.tile([P, 2 * BANK], BF16, tag="bank")
            for n, t in enumerate(tiles):
                nc.tensor.matmul(
                    out=picked[:, NODE_IN * n : NODE_IN * (n + 1)],
                    lhsT=pick[:, t - 1, :],
                    rhs=first[:, SRC],
                    start=True,
                    stop=True,
                )
            return picked

        def load_weight():
            nc.sync.dma_start(out=w_words[:].bitcast(I32), in_=Wt_words[0].bitcast(I32))
            for q in range(P // 32):
                nc.sync.dma_start(
                    out=w_scales[32 * q : 32 * q + LIVE_ROWS, :].bitcast(I32),
                    in_=Wt_scales[0, LIVE_ROWS * q : LIVE_ROWS * (q + 1), :].bitcast(I32),
                )

        def assemble_triplets():
            nc.vector.tensor_copy(
                out=later[:, :, SRC],
                in_=first[:, SRC].unsqueeze(1).to_broadcast([P, TILES - 1, NODE_IN]),
            )
            for t in range(1, TILES):
                picked = pick_destinations((t,))
                copy = nc.vector.tensor_copy if t == 1 else nc.scalar.copy
                copy(out=later[:, t - 1, DST], in_=picked[:, 0:NODE_IN])
            nc.vector.tensor_copy(out=later[:, :, EDGE], in_=first[:, D_IN:].rearrange("p (t f) -> p t f", f=EDGE_IN))

        def transpose_tile(t):
            words = (first[:, 0:D_IN] if t == 0 else later[:, t - 1, :]).bitcast(F32)
            flipped = psum.tile([P, BANK], F32, tag="bank")
            planes = flipped[:, 0:WORDS].rearrange("p (u m) -> p u m", u=2)
            for u in range(2):
                nc.tensor.transpose(planes[:, u, :], words[:, u:WORDS:2], identity[:])
            return planes

        def group_words(copy, planes):
            grouped = stage.tile([P, 4 * P], BF16, align_bytes=64)
            copy(
                out=grouped[:].bitcast(F32).rearrange("p (m u) -> p m u", u=2),
                in_=planes.rearrange("p u m -> p m u"),
            )
            return grouped

        def quantise_tile(t, grouped):
            nc.vector.quantize_mx(
                out=t_codes[:, t, :].bitcast(FP8X4), scales=t_scales[:, t, :], in_=grouped[:]
            )

        def multiply_tile(t, widths, after_second=None):
            first = 0
            for width in widths:
                last = first + width
                acc = psum.tile([P, BANK], F32, tag="bank")
                nc.tensor.matmul_mx(
                    out=acc[:, 0:width],
                    lhsT=t_codes[:, t, :].bitcast(FP8X4),
                    lhsT_scale=t_scales[:, t, :],
                    rhs=w_words[:, 2 * first : 2 * last].bitcast(FP4X4),
                    rhs_scale=w_scales[:, first:last],
                    start=True,
                    stop=True,
                )
                tenth = stage.tile([P, BANK], F32)
                nc.scalar.mul(out=tenth[:, 0:width], in_=acc[:, 0:width], mul=NEG_SLOPE)
                result = results.tile([P, BANK], F32)
                nc.vector.tensor_max(result[:, 0:width], acc[:, 0:width], tenth[:, 0:width])
                nc.sync.dma_start(out=out_rows[:, t, first:last], in_=result[:, 0:width])
                first = last
                if after_second is not None and last == 2 * P:
                    after_second()

        def keep_warm():
            unused = psum.tile([P, BANK], F32, tag="bank")
            nc.tensor.matmul(out=unused[:, 0:P], lhsT=idle_work[:], rhs=idle_work[:], start=True, stop=True)

        def warm_up():
            nc.gpsimd.memset(idle_work[:], 0.0)
            unused = psum.tile([P, BANK], F32, tag="bank")
            for _ in range(WARM_UP_PASSES):
                nc.tensor.matmul(out=unused[:, 0:P], lhsT=idle_work[:], rhs=idle_work[:], start=True, stop=True)

        def run():
            nc.vector.memset(w_scales[:].bitcast(I32), 0)
            warm_up()
            make_identity(nc, identity[:])
            make_picks()
            load_triplets()
            load_weight()
            assemble_triplets()
            planes = [transpose_tile(0)]
            keep_warm()
            planes += [transpose_tile(t) for t in range(1, TILES)]
            quantise_tile(0, group_words(nc.vector.tensor_copy, planes[0]))
            quantise_tile(1, group_words(nc.scalar.copy, planes[1]))
            grouped_2 = group_words(nc.scalar.copy, planes[2])
            grouped_3 = group_words(nc.vector.tensor_copy, planes[3])
            quantise_tile(2, grouped_2)
            multiply_tile(0, FIRST_TILE, after_second=lambda: quantise_tile(3, grouped_3))
            for t in range(1, TILES - 1):
                multiply_tile(t, MIDDLE_TILE)
            multiply_tile(TILES - 1, LAST_TILE)

        with tc.manual_schedule(engines={mybir.EngineType.PE, mybir.EngineType.DVE}):
            run()
